import numpy as np
import ml_dtypes


def mxq(x, axis, fmt="e4m3"):
    dtype, down = {"e4m3": (ml_dtypes.float8_e4m3fn, 7), "e5m2": (ml_dtypes.float8_e5m2, 14)}[fmt]
    v = np.moveaxis(np.asarray(x, np.float32).astype(ml_dtypes.bfloat16).astype(np.float64), axis, -1)
    blocks = v.reshape(v.shape[:-1] + (-1, 32))
    amax = np.abs(blocks).max(-1, keepdims=True)
    byte = np.maximum(np.where(amax > 0, np.frexp(amax)[1] - 1 + 127, 0) - down, 1)
    scale = np.exp2(byte - 127.0)
    codes = (blocks / scale).astype(np.float32).astype(dtype).astype(np.float64)
    return np.moveaxis((codes * scale).reshape(v.shape), -1, axis)


WIDE = False


def mx_kscale(k):
    if not WIDE:
        return np.ones(k)
    levels = np.array([10, -10, 5, -5, 0])
    a = np.random.permutation(np.resize(levels, k // 512 * 4)).reshape(k // 512, 4)
    idx = np.arange(k)
    return np.exp2(a[idx // 512, idx % 128 // 32])


BF16 = ml_dtypes.bfloat16


def bf(x):
    return np.asarray(x, np.float32).astype(BF16)


def f64(x):
    return np.asarray(x).astype(np.float64)


E2M1 = np.array([0.0, 0.5, 1.0, 1.5, 2.0, 3.0, 4.0, 6.0, -0.0, -0.5, -1.0, -1.5, -2.0, -3.0, -4.0, -6.0])


def pack_weight(w, fmt):
    k, n = w.shape
    w = f64(bf(w)).reshape(k // 32, 32, n)
    amax = np.abs(w).max(1)
    if fmt == "e4m3":
        byte = np.frexp(amax)[1] - 1 + 127 - 7
    else:
        mant, ex = np.frexp(amax / 6.0)
        byte = np.where(mant > 0.5, ex, ex - 1) + 127
    byte = np.clip(np.where(amax > 0, byte, 1), 1, 254)
    scaled = (w * np.exp2(127.0 - byte)[:, None, :]).reshape(k, n).astype(np.float32)
    by_word = np.ascontiguousarray(scaled.reshape(k // 512, 128, 4, n).transpose(0, 1, 3, 2))
    if fmt == "e4m3":
        words = by_word.astype(ml_dtypes.float8_e4m3fn).view(np.uint8)
    else:
        c = by_word.astype(ml_dtypes.float4_e2m1fn).view(np.uint8) & 0xF
        words = c[..., 0::2] | (c[..., 1::2] << 4)
    return np.ascontiguousarray(words), np.ascontiguousarray(byte.astype(np.uint8).reshape(k // 512, 16, n))


def unpack_weight(words, scales, fmt):
    g, p, n, _ = words.shape
    if fmt == "e4m3":
        vals = np.ascontiguousarray(words).view(ml_dtypes.float8_e4m3fn).astype(np.float64)
    else:
        nib = np.empty((g, p, n, 4), np.uint8)
        nib[..., 0::2] = words & 0xF
        nib[..., 1::2] = words >> 4
        vals = E2M1[nib]
    vals = vals * np.repeat(np.exp2(scales.astype(np.float64) - 127.0), 8, axis=1)[..., None]
    return vals.transpose(0, 1, 3, 2).reshape(g * 512, n)


E, F, H, MID, OUT = 128, 2048, 6144, 512, 2048
D = 2 * (F + H)
IN = D + 1
FMT = "e4m3"


def setup_inputs():
    s = mx_kscale(D)
    t = mx_kscale(MID)
    w1 = np.concatenate([np.random.standard_normal((MID, D)) / np.sqrt(D) / s[None, :],
                         np.random.standard_normal((MID, 1)) * 0.5], axis=1) * t[:, None]
    dst_node_feat = bf(np.random.standard_normal((E, F)) * s[:F])
    dst_node_hidden = bf(np.random.standard_normal((E, H)) * s[F:F + H])
    src_node_feat = bf(np.random.standard_normal((E, F)) * s[F + H:2 * F + H])
    src_node_hidden = bf(np.random.standard_normal((E, H)) * s[2 * F + H:])
    edge_feat = bf(np.random.standard_normal(E))
    b1 = bf(np.random.standard_normal(MID) * 0.3 * t)
    w2 = np.random.standard_normal((OUT, MID)) / np.sqrt(MID) / t[None, :]
    w2_words, w2_scales = pack_weight(np.ascontiguousarray(w2.T), FMT)
    b2 = bf(np.random.standard_normal(OUT) * 0.3)
    return {"dst_node_feat": dst_node_feat,
            "dst_node_hidden": dst_node_hidden,
            "src_node_feat": src_node_feat,
            "src_node_hidden": src_node_hidden,
            "edge_feat": edge_feat,
            "W1": bf(w1),
            "b1": b1,
            "W2_words": w2_words,
            "W2_scales": w2_scales,
            "b2": b2}


def reference(dst_node_feat, dst_node_hidden, src_node_feat, src_node_hidden, edge_feat, W1, b1, W2_words, W2_scales, b2):
    x = np.concatenate([f64(dst_node_feat), f64(dst_node_hidden), f64(src_node_feat), f64(src_node_hidden),
                        f64(edge_feat)[:, None]], axis=1)
    w1 = f64(W1)
    pre = (mxq(x[:, :D], 1, "e4m3") @ mxq(w1[:, :D], 1, "e4m3").T) + x[:, D:] * w1[:, D] + f64(b1)
    h = np.maximum(pre, 0.0)
    return np.tanh((mxq(h, 1, "e4m3") @ unpack_weight(W2_words, W2_scales, FMT)) + f64(b2))

@@ -1,0 +1,226 @@
+from contextlib import ExitStack
+
+import concourse.mybir as mybir
+from concourse.masks import make_identity
+
+F32 = mybir.dt.float32
+BF16 = mybir.dt.bfloat16
+I32 = mybir.dt.int32
+U32 = mybir.dt.uint32
+U8 = mybir.dt.uint8
+FP8X4 = mybir.dt.float8_e4m3fn_x4
+ADD = mybir.AluOpType.add
+MULT = mybir.AluOpType.mult
+TANH = mybir.ActivationFunctionType.Tanh
+
+P = 128
+PACK = 4
+K_PASS = P * PACK
+EDGES = 128
+NODE_K = 16384
+MID = 512
+OUT = 2048
+ROW_SETS = MID // P
+BANK = 512
+
+K_CHUNK = 2048
+K_ROUND = 2 * BANK
+ROUND_PASSES = K_ROUND // K_PASS
+CHUNK_ROUNDS = K_CHUNK // K_ROUND
+CHUNKS = NODE_K // K_CHUNK
+ROUNDS = NODE_K // K_ROUND
+RAW_BUFS = 6
+HALF = ROW_SETS * K_ROUND // 2
+
+FLOPS = 2 * EDGES * (NODE_K + 1) * MID + 2 * EDGES * MID * OUT
+
+
+def tile_edgenetwork_k_kernel(
+    tc,
+    dst_node_feat,
+    dst_node_hidden,
+    src_node_feat,
+    src_node_hidden,
+    edge_feat,
+    W1,
+    b1,
+    W2_words,
+    W2_scales,
+    b2,
+    out,
+):
+    nc = tc.nc
+    node_inputs = (dst_node_feat, dst_node_hidden, src_node_feat, src_node_hidden)
+    x_chunks = [part[:, k0 : k0 + K_CHUNK] for part in node_inputs for k0 in range(0, part.shape[1], K_CHUNK)]
+    w1_sets = W1.rearrange("(p t) k -> p t k", t=ROW_SETS)
+
+    with ExitStack() as stack:
+        const = stack.enter_context(tc.tile_pool(name="const", bufs=1))
+        raw = stack.enter_context(tc.tile_pool(name="raw", bufs=RAW_BUFS))
+        grouped = stack.enter_context(tc.tile_pool(name="grouped", bufs=3))
+        codes = stack.enter_context(tc.tile_pool(name="codes", bufs=3))
+        results = stack.enter_context(tc.tile_pool(name="results", bufs=2))
+        sums = stack.enter_context(tc.psum_pool(name="sums", bufs=1))
+        banks = stack.enter_context(tc.psum_pool(name="banks", bufs=4))
+        stack.enter_context(tc.manual_schedule())
+
+        x_raw = []
+        w_raw = []
+
+        def load_chunk(c):
+            x_tile = raw.tile([P, K_CHUNK], BF16)
+            nc.sync.dma_start(out=x_tile[:], in_=x_chunks[c])
+            x_raw.append(x_tile)
+            w_tile = raw.tile([P, ROW_SETS, K_CHUNK], BF16)
+            nc.sync.dma_start(out=w_tile[:], in_=w1_sets[:, :, c * K_CHUNK : (c + 1) * K_CHUNK])
+            w_raw.append(w_tile)
+
+        edge_all = const.tile([P, EDGES], BF16)
+        nc.scalar.dma_start(out=edge_all[:], in_=edge_feat.partition_broadcast(P))
+        b1_bf = const.tile([P, ROW_SETS], BF16)
+        nc.scalar.dma_start(out=b1_bf[:], in_=b1.rearrange("(p t) -> p t", t=ROW_SETS))
+        w1_edge_bf = const.tile([P, ROW_SETS, 1], BF16)
+        with nc.allow_non_contiguous_dma(reason="one column of W1: 512 single elements"):
+            nc.scalar.dma_start(out=w1_edge_bf[:], in_=w1_sets[:, :, NODE_K : NODE_K + 1])
+
+        b2_row = const.tile([P, OUT], BF16)
+        nc.vector.memset(b2_row[:].bitcast(I32), 0)
+        ones = const.tile([P, P], BF16)
+        nc.vector.memset(ones[:], 1.0)
+        w2_scales = const.tile([P, OUT], U8, align_bytes=64)
+        nc.vector.memset(w2_scales[:].bitcast(I32), 0)
+        warm = const.tile([P, 1], F32)
+        nc.vector.memset(warm[:], 0.0)
+        nc.scalar.activation(out=warm[:], in_=warm[:], func=TANH)
+        ident = const.tile([P, P], F32)
+        make_identity(nc, ident[:])
+
+        load_chunk(0)
+        nc.sync.dma_start(out=b2_row[0:1, :], in_=b2.unsqueeze(0))
+        for c in range(1, RAW_BUFS):
+            load_chunk(c)
+
+        b2_all = const.tile([P, OUT], BF16)
+        added = const.tile([P, ROW_SETS, EDGES], F32)
+
+        def prepare_biases():
+            for n in range(OUT // BANK):
+                cols = slice(n * BANK, (n + 1) * BANK)
+                spread = banks.tile([P, BANK], F32, tag="bank")
+                nc.tensor.matmul(out=spread[:], lhsT=ones[:], rhs=b2_row[:, cols], start=True, stop=True)
+                nc.vector.tensor_copy(out=b2_all[:, cols], in_=spread[:])
+            b1_f32 = const.tile([P, ROW_SETS], F32)
+            nc.vector.tensor_copy(out=b1_f32[:], in_=b1_bf[:])
+            w1_edge = const.tile([P, ROW_SETS], F32)
+            nc.vector.tensor_copy(out=w1_edge[:], in_=w1_edge_bf[:, :, 0])
+            for t in range(ROW_SETS):
+                nc.vector.tensor_scalar(
+                    out=added[:, t, :],
+                    in0=edge_all[:],
+                    scalar1=w1_edge[:, t : t + 1],
+                    scalar2=b1_f32[:, t : t + 1],
+                    op0=MULT,
+                    op1=ADD,
+                )
+
+        pre = [sums.tile([P, EDGES], F32, name="pre%d" % t) for t in range(ROW_SETS)]
+
+        def transpose_rows(row_pairs, grouped_pairs, copy):
+            bank = banks.tile([P, 2 * ROUND_PASSES, P], F32, tag="bank")
+            for b in range(2 * ROUND_PASSES):
+                nc.tensor.transpose(bank[:, b, :], row_pairs[:, b * P : (b + 1) * P], ident[:])
+            copy(
+                out=grouped_pairs.rearrange("p (g r u) -> p g r u", g=ROUND_PASSES, u=2),
+                in_=bank[:].rearrange("p (g u) r -> p g r u", u=2),
+            )
+
+        def transpose_round(r):
+            c, part = divmod(r, CHUNK_ROUNDS)
+            pairs = slice(part * BANK, (part + 1) * BANK)
+            x_grouped = grouped.tile([P, K_ROUND], BF16, align_bytes=64)
+            w_grouped = grouped.tile([P, ROW_SETS * K_ROUND], BF16, align_bytes=64)
+            transpose_rows(x_raw[c][:].bitcast(F32)[:, pairs], x_grouped[:].bitcast(F32), nc.vector.tensor_copy)
+            for t in range(ROW_SETS):
+                transpose_rows(
+                    w_raw[c][:, t, :].bitcast(F32)[:, pairs],
+                    w_grouped[:].bitcast(F32)[:, t * BANK : (t + 1) * BANK],
+                    nc.scalar.copy,
+                )
+            return x_grouped, w_grouped
+
+        def quantise_round(x_grouped, w_grouped):
+            x_codes = codes.tile([P, K_ROUND // PACK], U32, align_bytes=64)
+            x_scales = codes.tile([P, K_ROUND // PACK], U8, align_bytes=64)
+            nc.vector.quantize_mx(out=x_codes[:].bitcast(FP8X4), scales=x_scales[:], in_=x_grouped[:])
+            w_codes = codes.tile([P, ROW_SETS * K_ROUND // PACK], U32, align_bytes=64)
+            w_scales = codes.tile([P, ROW_SETS * K_ROUND // PACK], U8, align_bytes=64)
+            for half in range(2):
+                words = slice(half * HALF // PACK, (half + 1) * HALF // PACK)
+                nc.vector.quantize_mx(
+                    out=w_codes[:, words].bitcast(FP8X4),
+                    scales=w_scales[:, words],
+                    in_=w_grouped[:, half * HALF : (half + 1) * HALF],
+                )
+            return x_codes, x_scales, w_codes, w_scales
+
+        def multiply_round(r, x_codes, x_scales, w_codes, w_scales):
+            for t in range(ROW_SETS):
+                for g in range(ROUND_PASSES):
+                    w_cols = slice((t * ROUND_PASSES + g) * P, (t * ROUND_PASSES + g + 1) * P)
+                    x_cols = slice(g * EDGES, (g + 1) * EDGES)
+                    nc.tensor.matmul_mx(
+                        out=pre[t][:],
+                        lhsT=w_codes[:, w_cols].bitcast(FP8X4),
+                        lhsT_scale=w_scales[:, w_cols],
+                        rhs=x_codes[:, x_cols].bitcast(FP8X4),
+                        rhs_scale=x_scales[:, x_cols],
+                        start=(r == 0 and g == 0),
+                        stop=(r == ROUNDS - 1 and g == ROUND_PASSES - 1),
+                    )
+
+        for r in range(ROUNDS):
+            x_grouped, w_grouped = transpose_round(r)
+            c, part = divmod(r, CHUNK_ROUNDS)
+            if part == CHUNK_ROUNDS - 1 and c + RAW_BUFS < CHUNKS:
+                load_chunk(c + RAW_BUFS)
+            if r == 0:
+                prepare_biases()
+            else:
+                multiply_round(r - 1, *quantised)
+            quantised = quantise_round(x_grouped, w_grouped)
+        multiply_round(ROUNDS - 1, *quantised)
+
+        scale_rows = W2_scales[0].rearrange("(q r) n -> r q n", r=4)
+        for r in range(4):
+            nc.sync.dma_start(out=w2_scales[r:P:32, :].bitcast(I32), in_=scale_rows[r].bitcast(I32))
+        w2_codes = const.tile([P, OUT], U32, align_bytes=64)
+        nc.sync.dma_start(out=w2_codes[:].bitcast(I32), in_=W2_words[0].rearrange("p n t -> p (n t)").bitcast(I32))
+
+        h_f32 = const.tile([P, ROW_SETS, EDGES], F32)
+        for t in range(ROW_SETS):
+            nc.vector.tensor_tensor(out=h_f32[:, t, :], in0=pre[t][:], in1=added[:, t, :], op=ADD)
+        h_grouped = const.tile([P, EDGES, PACK], BF16, align_bytes=64)
+        nc.vector.tensor_scalar_max(out=h_grouped[:], in0=h_f32[:].rearrange("p t e -> p e t"), scalar1=0.0)
+        h_codes = const.tile([P, EDGES], U32, align_bytes=64)
+        h_scales = const.tile([P, EDGES], U8, align_bytes=64)
+        nc.vector.quantize_mx(
+            out=h_codes[:].bitcast(FP8X4), scales=h_scales[:], in_=h_grouped[:].rearrange("p e t -> p (e t)")
+        )
+
+        for n in range(OUT // BANK):
+            cols = slice(n * BANK, (n + 1) * BANK)
+            product = banks.tile([P, BANK], F32, tag="bank")
+            nc.tensor.matmul_mx(
+                out=product[:],
+                lhsT=h_codes[:].bitcast(FP8X4),
+                lhsT_scale=h_scales[:],
+                rhs=w2_codes[:, cols].bitcast(FP8X4),
+                rhs_scale=w2_scales[:, cols],
+                start=True,
+                stop=True,
+            )
+            biased = results.tile([P, BANK], F32)
+            nc.vector.tensor_tensor(out=biased[:], in0=product[:], in1=b2_all[:, cols], op=ADD)
+            y = results.tile([P, BANK], F32)
+            nc.scalar.activation(out=y[:], in_=biased[:], func=TANH)
+            nc.sync.dma_start(out=out[:, cols], in_=y[:])

@@ -10,27 +10,29 @@ U32 = mybir.dt.uint32
 U8 = mybir.dt.uint8
 FP8X4 = mybir.dt.float8_e4m3fn_x4
 ADD = mybir.AluOpType.add
-MULT = mybir.AluOpType.mult
+RELU = mybir.ActivationFunctionType.Relu
 TANH = mybir.ActivationFunctionType.Tanh
 
 P = 128
 PACK = 4
 K_PASS = P * PACK
+PASS_PAIRS = K_PASS // 2
 EDGES = 128
 NODE_K = 16384
 MID = 512
 OUT = 2048
 ROW_SETS = MID // P
 BANK = 512
+PSUM_BANKS = 8
 
 K_CHUNK = 2048
-K_ROUND = 2 * BANK
-ROUND_PASSES = K_ROUND // K_PASS
+ROUND_PASSES = 2
+K_ROUND = ROUND_PASSES * K_PASS
 CHUNK_ROUNDS = K_CHUNK // K_ROUND
 CHUNKS = NODE_K // K_CHUNK
 ROUNDS = NODE_K // K_ROUND
 RAW_BUFS = 6
-HALF = ROW_SETS * K_ROUND // 2
+MX_LAG = 2
 
 FLOPS = 2 * EDGES * (NODE_K + 1) * MID + 2 * EDGES * MID * OUT
 
@@ -52,16 +54,16 @@ def tile_edgenetwork_k_kernel(
     nc = tc.nc
     node_inputs = (dst_node_feat, dst_node_hidden, src_node_feat, src_node_hidden)
     x_chunks = [part[:, k0 : k0 + K_CHUNK] for part in node_inputs for k0 in range(0, part.shape[1], K_CHUNK)]
-    w1_sets = W1.rearrange("(p t) k -> p t k", t=ROW_SETS)
+    w1_sets = W1.rearrange("(s r) k -> r s k", s=ROW_SETS)
 
     with ExitStack() as stack:
         const = stack.enter_context(tc.tile_pool(name="const", bufs=1))
         raw = stack.enter_context(tc.tile_pool(name="raw", bufs=RAW_BUFS))
         grouped = stack.enter_context(tc.tile_pool(name="grouped", bufs=3))
-        codes = stack.enter_context(tc.tile_pool(name="codes", bufs=3))
+        codes = stack.enter_context(tc.tile_pool(name="codes", bufs=MX_LAG + 2))
         results = stack.enter_context(tc.tile_pool(name="results", bufs=2))
         sums = stack.enter_context(tc.psum_pool(name="sums", bufs=1))
-        banks = stack.enter_context(tc.psum_pool(name="banks", bufs=4))
+        banks = stack.enter_context(tc.psum_pool(name="banks", bufs=PSUM_BANKS - 1))
         stack.enter_context(tc.manual_schedule())
 
         x_raw = []
@@ -75,18 +77,11 @@ def tile_edgenetwork_k_kernel(
             nc.sync.dma_start(out=w_tile[:], in_=w1_sets[:, :, c * K_CHUNK : (c + 1) * K_CHUNK])
             w_raw.append(w_tile)
 
-        edge_all = const.tile([P, EDGES], BF16)
-        nc.scalar.dma_start(out=edge_all[:], in_=edge_feat.partition_broadcast(P))
-        b1_bf = const.tile([P, ROW_SETS], BF16)
-        nc.scalar.dma_start(out=b1_bf[:], in_=b1.rearrange("(p t) -> p t", t=ROW_SETS))
-        w1_edge_bf = const.tile([P, ROW_SETS, 1], BF16)
-        with nc.allow_non_contiguous_dma(reason="one column of W1: 512 single elements"):
-            nc.scalar.dma_start(out=w1_edge_bf[:], in_=w1_sets[:, :, NODE_K : NODE_K + 1])
-
-        b2_row = const.tile([P, OUT], BF16)
-        nc.vector.memset(b2_row[:].bitcast(I32), 0)
-        ones = const.tile([P, P], BF16)
-        nc.vector.memset(ones[:], 1.0)
+        bias_rows = const.tile([P, MID + OUT], BF16)
+        nc.vector.memset(bias_rows[:].bitcast(I32), 0)
+        bias_lhsT = const.tile([P, EDGES], BF16)
+        nc.vector.memset(bias_lhsT[:], 0.0)
+        nc.vector.memset(bias_lhsT[0:1, :], 1.0)
         w2_scales = const.tile([P, OUT], U8, align_bytes=64)
         nc.vector.memset(w2_scales[:].bitcast(I32), 0)
         warm = const.tile([P, 1], F32)
@@ -96,99 +91,108 @@ def tile_edgenetwork_k_kernel(
         make_identity(nc, ident[:])
 
         load_chunk(0)
-        nc.sync.dma_start(out=b2_row[0:1, :], in_=b2.unsqueeze(0))
+        nc.sync.dma_start(out=bias_lhsT[1:2, :], in_=edge_feat.unsqueeze(0))
+        nc.sync.dma_start(out=bias_rows[0:1, 0:MID], in_=b1.unsqueeze(0))
+        nc.sync.dma_start(out=bias_rows[0:1, MID : MID + OUT], in_=b2.unsqueeze(0))
+        with nc.allow_non_contiguous_dma(reason="one column of W1: 512 single elements"):
+            nc.sync.dma_start(out=bias_rows[1:2, 0:MID], in_=W1[:, NODE_K : NODE_K + 1].rearrange("m o -> o m"))
         for c in range(1, RAW_BUFS):
             load_chunk(c)
 
+        added = const.tile([P, PACK, P], F32)
         b2_all = const.tile([P, OUT], BF16)
-        added = const.tile([P, ROW_SETS, EDGES], F32)
 
         def prepare_biases():
+            spread = banks.tile([P, BANK], F32, tag="bank")
+            nc.tensor.matmul(out=spread[:], lhsT=bias_lhsT[:], rhs=bias_rows[:, 0:MID], start=True, stop=True)
+            nc.vector.tensor_copy(out=added[:], in_=spread[:].rearrange("e (p t) -> e t p", t=PACK))
             for n in range(OUT // BANK):
                 cols = slice(n * BANK, (n + 1) * BANK)
                 spread = banks.tile([P, BANK], F32, tag="bank")
-                nc.tensor.matmul(out=spread[:], lhsT=ones[:], rhs=b2_row[:, cols], start=True, stop=True)
-                nc.vector.tensor_copy(out=b2_all[:, cols], in_=spread[:])
-            b1_f32 = const.tile([P, ROW_SETS], F32)
-            nc.vector.tensor_copy(out=b1_f32[:], in_=b1_bf[:])
-            w1_edge = const.tile([P, ROW_SETS], F32)
-            nc.vector.tensor_copy(out=w1_edge[:], in_=w1_edge_bf[:, :, 0])
-            for t in range(ROW_SETS):
-                nc.vector.tensor_scalar(
-                    out=added[:, t, :],
-                    in0=edge_all[:],
-                    scalar1=w1_edge[:, t : t + 1],
-                    scalar2=b1_f32[:, t : t + 1],
-                    op0=MULT,
-                    op1=ADD,
+                nc.tensor.matmul(
+                    out=spread[:], lhsT=bias_lhsT[:], rhs=bias_rows[:, MID + n * BANK : MID + (n + 1) * BANK],
+                    start=True, stop=True,
                 )
+                nc.vector.tensor_copy(out=b2_all[:, cols], in_=spread[:])
 
-        pre = [sums.tile([P, EDGES], F32, name="pre%d" % t) for t in range(ROW_SETS)]
+        pre = sums.tile([P, MID], F32)
 
-        def transpose_rows(row_pairs, grouped_pairs, copy):
-            bank = banks.tile([P, 2 * ROUND_PASSES, P], F32, tag="bank")
-            for b in range(2 * ROUND_PASSES):
-                nc.tensor.transpose(bank[:, b, :], row_pairs[:, b * P : (b + 1) * P], ident[:])
+        def to_partitions(blocks, grouped_pairs, copy):
+            bank = banks.tile([P, 4, P], F32, tag="bank")
+            for b, block in enumerate(blocks):
+                nc.tensor.transpose(bank[:, b, :], block, ident[:])
             copy(
-                out=grouped_pairs.rearrange("p (g r u) -> p g r u", g=ROUND_PASSES, u=2),
-                in_=bank[:].rearrange("p (g u) r -> p g r u", u=2),
+                out=grouped_pairs.rearrange("p (a r u) -> p a r u", a=2, u=2),
+                in_=bank[:].rearrange("p (a u) r -> p a r u", u=2),
             )
 
         def transpose_round(r):
             c, part = divmod(r, CHUNK_ROUNDS)
-            pairs = slice(part * BANK, (part + 1) * BANK)
-            x_grouped = grouped.tile([P, K_ROUND], BF16, align_bytes=64)
-            w_grouped = grouped.tile([P, ROW_SETS * K_ROUND], BF16, align_bytes=64)
-            transpose_rows(x_raw[c][:].bitcast(F32)[:, pairs], x_grouped[:].bitcast(F32), nc.vector.tensor_copy)
-            for t in range(ROW_SETS):
-                transpose_rows(
-                    w_raw[c][:, t, :].bitcast(F32)[:, pairs],
-                    w_grouped[:].bitcast(F32)[:, t * BANK : (t + 1) * BANK],
-                    nc.scalar.copy,
-                )
+            x_pairs = x_raw[c][:].bitcast(F32)
+            w_pairs = w_raw[c][:].bitcast(F32)
+            first = part * ROUND_PASSES * PASS_PAIRS
+
+            def block(g, u):
+                return slice(first + g * PASS_PAIRS + u * P, first + g * PASS_PAIRS + (u + 1) * P)
+
+            x_grouped = grouped.tile([P, ROUND_PASSES * EDGES * PACK], BF16, align_bytes=64)
+            w_grouped = grouped.tile([P, ROUND_PASSES * MID * PACK], BF16, align_bytes=64)
+            to_partitions(
+                [x_pairs[:, block(g, u)] for g in range(ROUND_PASSES) for u in range(2)],
+                x_grouped[:].bitcast(F32),
+                nc.vector.tensor_copy,
+            )
+            for g in range(ROUND_PASSES):
+                for s in range(0, ROW_SETS, 2):
+                    to_partitions(
+                        [w_pairs[:, s + a, block(g, u)] for a in range(2) for u in range(2)],
+                        w_grouped[:].bitcast(F32)[:, (g * ROW_SETS + s) * 2 * P : (g * ROW_SETS + s + 2) * 2 * P],
+                        nc.scalar.copy,
+                    )
             return x_grouped, w_grouped
 
         def quantise_round(x_grouped, w_grouped):
-            x_codes = codes.tile([P, K_ROUND // PACK], U32, align_bytes=64)
-            x_scales = codes.tile([P, K_ROUND // PACK], U8, align_bytes=64)
-            nc.vector.quantize_mx(out=x_codes[:].bitcast(FP8X4), scales=x_scales[:], in_=x_grouped[:])
-            w_codes = codes.tile([P, ROW_SETS * K_ROUND // PACK], U32, align_bytes=64)
-            w_scales = codes.tile([P, ROW_SETS * K_ROUND // PACK], U8, align_bytes=64)
-            for half in range(2):
-                words = slice(half * HALF // PACK, (half + 1) * HALF // PACK)
+            x_codes = codes.tile([P, ROUND_PASSES * EDGES], U32, align_bytes=64)
+            x_scales = codes.tile([P, ROUND_PASSES * EDGES], U8, align_bytes=64)
+            w_codes = codes.tile([P, ROUND_PASSES * MID], U32, align_bytes=64)
+            w_scales = codes.tile([P, ROUND_PASSES * MID], U8, align_bytes=64)
+
+            def quantise_w(g):
                 nc.vector.quantize_mx(
-                    out=w_codes[:, words].bitcast(FP8X4),
-                    scales=w_scales[:, words],
-                    in_=w_grouped[:, half * HALF : (half + 1) * HALF],
+                    out=w_codes[:, g * MID : (g + 1) * MID].bitcast(FP8X4),
+                    scales=w_scales[:, g * MID : (g + 1) * MID],
+                    in_=w_grouped[:, g * MID * PACK : (g + 1) * MID * PACK],
                 )
+
+            quantise_w(0)
+            nc.vector.quantize_mx(out=x_codes[:].bitcast(FP8X4), scales=x_scales[:], in_=x_grouped[:])
+            quantise_w(1)
             return x_codes, x_scales, w_codes, w_scales
 
         def multiply_round(r, x_codes, x_scales, w_codes, w_scales):
-            for t in range(ROW_SETS):
-                for g in range(ROUND_PASSES):
-                    w_cols = slice((t * ROUND_PASSES + g) * P, (t * ROUND_PASSES + g + 1) * P)
-                    x_cols = slice(g * EDGES, (g + 1) * EDGES)
-                    nc.tensor.matmul_mx(
-                        out=pre[t][:],
-                        lhsT=w_codes[:, w_cols].bitcast(FP8X4),
-                        lhsT_scale=w_scales[:, w_cols],
-                        rhs=x_codes[:, x_cols].bitcast(FP8X4),
-                        rhs_scale=x_scales[:, x_cols],
-                        start=(r == 0 and g == 0),
-                        stop=(r == ROUNDS - 1 and g == ROUND_PASSES - 1),
-                    )
+            for g in range(ROUND_PASSES):
+                nc.tensor.matmul_mx(
+                    out=pre[:],
+                    lhsT=x_codes[:, g * EDGES : (g + 1) * EDGES].bitcast(FP8X4),
+                    lhsT_scale=x_scales[:, g * EDGES : (g + 1) * EDGES],
+                    rhs=w_codes[:, g * MID : (g + 1) * MID].bitcast(FP8X4),
+                    rhs_scale=w_scales[:, g * MID : (g + 1) * MID],
+                    start=(r == 0 and g == 0),
+                    stop=(r == ROUNDS - 1 and g == ROUND_PASSES - 1),
+                )
 
-        for r in range(ROUNDS):
-            x_grouped, w_grouped = transpose_round(r)
-            c, part = divmod(r, CHUNK_ROUNDS)
-            if part == CHUNK_ROUNDS - 1 and c + RAW_BUFS < CHUNKS:
-                load_chunk(c + RAW_BUFS)
+        quantised = []
+        for r in range(ROUNDS + MX_LAG):
+            if r < ROUNDS:
+                x_grouped, w_grouped = transpose_round(r)
+                quantised.append(quantise_round(x_grouped, w_grouped))
+                c, part = divmod(r, CHUNK_ROUNDS)
+                if part == CHUNK_ROUNDS - 1 and c + RAW_BUFS < CHUNKS:
+                    load_chunk(c + RAW_BUFS)
             if r == 0:
                 prepare_biases()
-            else:
-                multiply_round(r - 1, *quantised)
-            quantised = quantise_round(x_grouped, w_grouped)
-        multiply_round(ROUNDS - 1, *quantised)
+            if r >= MX_LAG:
+                multiply_round(r - MX_LAG, *quantised[r - MX_LAG])
 
         scale_rows = W2_scales[0].rearrange("(q r) n -> r q n", r=4)
         for r in range(4):
@@ -196,11 +200,13 @@ def tile_edgenetwork_k_kernel(
         w2_codes = const.tile([P, OUT], U32, align_bytes=64)
         nc.sync.dma_start(out=w2_codes[:].bitcast(I32), in_=W2_words[0].rearrange("p n t -> p (n t)").bitcast(I32))
 
-        h_f32 = const.tile([P, ROW_SETS, EDGES], F32)
-        for t in range(ROW_SETS):
-            nc.vector.tensor_tensor(out=h_f32[:, t, :], in0=pre[t][:], in1=added[:, t, :], op=ADD)
+        h_rows = const.tile([P, PACK, P], F32)
+        nc.vector.tensor_tensor(out=h_rows[:], in0=pre[:].rearrange("e (p t) -> e t p", t=PACK), in1=added[:], op=ADD)
+        h_bank = banks.tile([P, PACK, EDGES], F32, tag="bank")
+        for t in range(PACK):
+            nc.tensor.transpose(h_bank[:, t, :], h_rows[:, t, :], ident[:])
         h_grouped = const.tile([P, EDGES, PACK], BF16, align_bytes=64)
-        nc.vector.tensor_scalar_max(out=h_grouped[:], in0=h_f32[:].rearrange("p t e -> p e t"), scalar1=0.0)
+        nc.scalar.activation(out=h_grouped[:], in_=h_bank[:].rearrange("p t e -> p e t"), func=RELU)
         h_codes = const.tile([P, EDGES], U32, align_bytes=64)
         h_scales = const.tile([P, EDGES], U8, align_bytes=64)
         nc.vector.quantize_mx(

@@ -10,13 +10,13 @@ U32 = mybir.dt.uint32
 U8 = mybir.dt.uint8
 FP8X4 = mybir.dt.float8_e4m3fn_x4
 ADD = mybir.AluOpType.add
+MULT = mybir.AluOpType.mult
 RELU = mybir.ActivationFunctionType.Relu
 TANH = mybir.ActivationFunctionType.Tanh
 
 P = 128
 PACK = 4
 K_PASS = P * PACK
-PASS_PAIRS = K_PASS // 2
 EDGES = 128
 NODE_K = 16384
 MID = 512
@@ -25,14 +25,14 @@ ROW_SETS = MID // P
 BANK = 512
 PSUM_BANKS = 8
 
-K_CHUNK = 2048
-ROUND_PASSES = 2
-K_ROUND = ROUND_PASSES * K_PASS
-CHUNK_ROUNDS = K_CHUNK // K_ROUND
-CHUNKS = NODE_K // K_CHUNK
-ROUNDS = NODE_K // K_ROUND
-RAW_BUFS = 6
-MX_LAG = 2
+K_BANK = 2 * BANK
+BANK_PASSES = K_BANK // K_PASS
+UNIT_BANKS = 4
+K_UNIT = UNIT_BANKS * K_BANK
+UNIT_PASSES = K_UNIT // K_PASS
+ROW_UNITS = NODE_K // K_UNIT
+W_UNITS = ROW_SETS * ROW_UNITS
+W_BUFS = 8
 
 FLOPS = 2 * EDGES * (NODE_K + 1) * MID + 2 * EDGES * MID * OUT
 
@@ -53,35 +53,32 @@ def tile_edgenetwork_k_kernel(
 ):
     nc = tc.nc
     node_inputs = (dst_node_feat, dst_node_hidden, src_node_feat, src_node_hidden)
-    x_chunks = [part[:, k0 : k0 + K_CHUNK] for part in node_inputs for k0 in range(0, part.shape[1], K_CHUNK)]
-    w1_sets = W1.rearrange("(s r) k -> r s k", s=ROW_SETS)
+    w1_sets = W1.rearrange("(p t) k -> t p k", t=ROW_SETS)
 
     with ExitStack() as stack:
         const = stack.enter_context(tc.tile_pool(name="const", bufs=1))
-        raw = stack.enter_context(tc.tile_pool(name="raw", bufs=RAW_BUFS))
-        grouped = stack.enter_context(tc.tile_pool(name="grouped", bufs=3))
-        codes = stack.enter_context(tc.tile_pool(name="codes", bufs=MX_LAG + 2))
-        results = stack.enter_context(tc.tile_pool(name="results", bufs=2))
+        raw = stack.enter_context(tc.tile_pool(name="raw", bufs=W_BUFS))
+        grouped_pool = stack.enter_context(tc.tile_pool(name="grouped", bufs=3))
+        codes = stack.enter_context(tc.tile_pool(name="codes", bufs=3))
+        results = stack.enter_context(tc.tile_pool(name="results", bufs=OUT // BANK))
         sums = stack.enter_context(tc.psum_pool(name="sums", bufs=1))
         banks = stack.enter_context(tc.psum_pool(name="banks", bufs=PSUM_BANKS - 1))
         stack.enter_context(tc.manual_schedule())
 
-        x_raw = []
-        w_raw = []
+        edge_all = const.tile([P, EDGES], BF16)
+        nc.scalar.dma_start(out=edge_all[:], in_=edge_feat.partition_broadcast(P))
+        b1_bf = const.tile([P, ROW_SETS], BF16)
+        nc.scalar.dma_start(out=b1_bf[:], in_=b1.rearrange("(p t) -> p t", t=ROW_SETS))
+        w1_edge_bf = const.tile([P, ROW_SETS, 1], BF16)
+        with nc.allow_non_contiguous_dma(reason="one column of W1: 512 single elements"):
+            nc.scalar.dma_start(
+                out=w1_edge_bf[:], in_=W1.rearrange("(p t) k -> p t k", t=ROW_SETS)[:, :, NODE_K : NODE_K + 1]
+            )
 
-        def load_chunk(c):
-            x_tile = raw.tile([P, K_CHUNK], BF16)
-            nc.sync.dma_start(out=x_tile[:], in_=x_chunks[c])
-            x_raw.append(x_tile)
-            w_tile = raw.tile([P, ROW_SETS, K_CHUNK], BF16)
-            nc.sync.dma_start(out=w_tile[:], in_=w1_sets[:, :, c * K_CHUNK : (c + 1) * K_CHUNK])
-            w_raw.append(w_tile)
-
-        bias_rows = const.tile([P, MID + OUT], BF16)
-        nc.vector.memset(bias_rows[:].bitcast(I32), 0)
-        bias_lhsT = const.tile([P, EDGES], BF16)
-        nc.vector.memset(bias_lhsT[:], 0.0)
-        nc.vector.memset(bias_lhsT[0:1, :], 1.0)
+        b2_row = const.tile([P, OUT], BF16)
+        nc.vector.memset(b2_row[:].bitcast(I32), 0)
+        ones = const.tile([P, P], BF16)
+        nc.vector.memset(ones[:], 1.0)
         w2_scales = const.tile([P, OUT], U8, align_bytes=64)
         nc.vector.memset(w2_scales[:].bitcast(I32), 0)
         warm = const.tile([P, 1], F32)
@@ -90,109 +87,113 @@ def tile_edgenetwork_k_kernel(
         ident = const.tile([P, P], F32)
         make_identity(nc, ident[:])
 
-        load_chunk(0)
-        nc.sync.dma_start(out=bias_lhsT[1:2, :], in_=edge_feat.unsqueeze(0))
-        nc.sync.dma_start(out=bias_rows[0:1, 0:MID], in_=b1.unsqueeze(0))
-        nc.sync.dma_start(out=bias_rows[0:1, MID : MID + OUT], in_=b2.unsqueeze(0))
-        with nc.allow_non_contiguous_dma(reason="one column of W1: 512 single elements"):
-            nc.sync.dma_start(out=bias_rows[1:2, 0:MID], in_=W1[:, NODE_K : NODE_K + 1].rearrange("m o -> o m"))
-        for c in range(1, RAW_BUFS):
-            load_chunk(c)
+        x_banks = []
+        for i, part in enumerate(node_inputs):
+            x_tile = const.tile([P, part.shape[1]], BF16, name="x_raw%d" % i)
+            nc.sync.dma_start(out=x_tile[:], in_=part)
+            x_banks.extend([x_tile[:].bitcast(F32)[:, j * BANK : (j + 1) * BANK] for j in range(part.shape[1] // K_BANK)])
+            if i == 0:
+                nc.sync.dma_start(out=b2_row[0:1, :], in_=b2.unsqueeze(0))
 
-        added = const.tile([P, PACK, P], F32)
+        w_raw = []
+
+        def load_w_unit(u):
+            t, kq = divmod(u, ROW_UNITS)
+            w_tile = raw.tile([P, K_UNIT], BF16)
+            nc.sync.dma_start(out=w_tile[:], in_=w1_sets[t][:, kq * K_UNIT : (kq + 1) * K_UNIT])
+            w_raw.append(w_tile)
+
+        for u in range(W_BUFS):
+            load_w_unit(u)
+
+        def quantise_unit(bank_pairs, unit_codes, unit_scales):
+            grouped = grouped_pool.tile([P, K_UNIT], BF16, align_bytes=64)
+            for j, pairs in enumerate(bank_pairs):
+                bank = banks.tile([P, 2 * BANK_PASSES, P], F32, tag="bank")
+                for b in range(2 * BANK_PASSES):
+                    nc.tensor.transpose(bank[:, b, :], pairs[:, b * P : (b + 1) * P], ident[:])
+                copy = nc.vector.tensor_copy if j == 0 else nc.scalar.copy
+                copy(
+                    out=grouped[:].bitcast(F32)[:, j * BANK : (j + 1) * BANK].rearrange(
+                        "p (g r u) -> p g r u", g=BANK_PASSES, u=2
+                    ),
+                    in_=bank[:].rearrange("p (g u) r -> p g r u", u=2),
+                )
+            for half in range(2):
+                words = slice(half * K_UNIT // PACK // 2, (half + 1) * K_UNIT // PACK // 2)
+                nc.vector.quantize_mx(
+                    out=unit_codes[:, words].bitcast(FP8X4),
+                    scales=unit_scales[:, words],
+                    in_=grouped[:, half * K_UNIT // 2 : (half + 1) * K_UNIT // 2],
+                )
+
         b2_all = const.tile([P, OUT], BF16)
+        added = const.tile([P, ROW_SETS, EDGES], F32)
 
         def prepare_biases():
-            spread = banks.tile([P, BANK], F32, tag="bank")
-            nc.tensor.matmul(out=spread[:], lhsT=bias_lhsT[:], rhs=bias_rows[:, 0:MID], start=True, stop=True)
-            nc.vector.tensor_copy(out=added[:], in_=spread[:].rearrange("e (p t) -> e t p", t=PACK))
             for n in range(OUT // BANK):
                 cols = slice(n * BANK, (n + 1) * BANK)
                 spread = banks.tile([P, BANK], F32, tag="bank")
-                nc.tensor.matmul(
-                    out=spread[:], lhsT=bias_lhsT[:], rhs=bias_rows[:, MID + n * BANK : MID + (n + 1) * BANK],
-                    start=True, stop=True,
-                )
+                nc.tensor.matmul(out=spread[:], lhsT=ones[:], rhs=b2_row[:, cols], start=True, stop=True)
                 nc.vector.tensor_copy(out=b2_all[:, cols], in_=spread[:])
-
-        pre = sums.tile([P, MID], F32)
-
-        def to_partitions(blocks, grouped_pairs, copy):
-            bank = banks.tile([P, 4, P], F32, tag="bank")
-            for b, block in enumerate(blocks):
-                nc.tensor.transpose(bank[:, b, :], block, ident[:])
-            copy(
-                out=grouped_pairs.rearrange("p (a r u) -> p a r u", a=2, u=2),
-                in_=bank[:].rearrange("p (a u) r -> p a r u", u=2),
-            )
-
-        def transpose_round(r):
-            c, part = divmod(r, CHUNK_ROUNDS)
-            x_pairs = x_raw[c][:].bitcast(F32)
-            w_pairs = w_raw[c][:].bitcast(F32)
-            first = part * ROUND_PASSES * PASS_PAIRS
-
-            def block(g, u):
-                return slice(first + g * PASS_PAIRS + u * P, first + g * PASS_PAIRS + (u + 1) * P)
-
-            x_grouped = grouped.tile([P, ROUND_PASSES * EDGES * PACK], BF16, align_bytes=64)
-            w_grouped = grouped.tile([P, ROUND_PASSES * MID * PACK], BF16, align_bytes=64)
-            to_partitions(
-                [x_pairs[:, block(g, u)] for g in range(ROUND_PASSES) for u in range(2)],
-                x_grouped[:].bitcast(F32),
-                nc.vector.tensor_copy,
-            )
-            for g in range(ROUND_PASSES):
-                for s in range(0, ROW_SETS, 2):
-                    to_partitions(
-                        [w_pairs[:, s + a, block(g, u)] for a in range(2) for u in range(2)],
-                        w_grouped[:].bitcast(F32)[:, (g * ROW_SETS + s) * 2 * P : (g * ROW_SETS + s + 2) * 2 * P],
-                        nc.scalar.copy,
-                    )
-            return x_grouped, w_grouped
-
-        def quantise_round(x_grouped, w_grouped):
-            x_codes = codes.tile([P, ROUND_PASSES * EDGES], U32, align_bytes=64)
-            x_scales = codes.tile([P, ROUND_PASSES * EDGES], U8, align_bytes=64)
-            w_codes = codes.tile([P, ROUND_PASSES * MID], U32, align_bytes=64)
-            w_scales = codes.tile([P, ROUND_PASSES * MID], U8, align_bytes=64)
-
-            def quantise_w(g):
-                nc.vector.quantize_mx(
-                    out=w_codes[:, g * MID : (g + 1) * MID].bitcast(FP8X4),
-                    scales=w_scales[:, g * MID : (g + 1) * MID],
-                    in_=w_grouped[:, g * MID * PACK : (g + 1) * MID * PACK],
+            b1_f32 = const.tile([P, ROW_SETS], F32)
+            nc.vector.tensor_copy(out=b1_f32[:], in_=b1_bf[:])
+            w1_edge = const.tile([P, ROW_SETS], F32)
+            nc.vector.tensor_copy(out=w1_edge[:], in_=w1_edge_bf[:, :, 0])
+            for t in range(ROW_SETS):
+                nc.vector.tensor_scalar(
+                    out=added[:, t, :],
+                    in0=edge_all[:],
+                    scalar1=w1_edge[:, t : t + 1],
+                    scalar2=b1_f32[:, t : t + 1],
+                    op0=MULT,
+                    op1=ADD,
                 )
 
-            quantise_w(0)
-            nc.vector.quantize_mx(out=x_codes[:].bitcast(FP8X4), scales=x_scales[:], in_=x_grouped[:])
-            quantise_w(1)
-            return x_codes, x_scales, w_codes, w_scales
+        x_codes = []
+        x_scales = []
+        for kq in range(ROW_UNITS):
+            x_unit_codes = const.tile([P, K_UNIT // PACK], U32, name="x_codes%d" % kq, align_bytes=64)
+            x_unit_scales = const.tile([P, K_UNIT // PACK], U8, name="x_scales%d" % kq, align_bytes=64)
+            quantise_unit(x_banks[kq * UNIT_BANKS : (kq + 1) * UNIT_BANKS], x_unit_codes, x_unit_scales)
+            x_codes.append(x_unit_codes)
+            x_scales.append(x_unit_scales)
+            if kq == 0:
+                prepare_biases()
 
-        def multiply_round(r, x_codes, x_scales, w_codes, w_scales):
-            for g in range(ROUND_PASSES):
+        pre = sums.tile([P, ROW_SETS, EDGES], F32)
+        h_grouped = const.tile([P, EDGES, PACK], BF16, align_bytes=64)
+
+        def multiply_unit(u, w_codes, w_scales):
+            t, kq = divmod(u, ROW_UNITS)
+            for i in range(UNIT_PASSES):
+                cols = slice(i * P, (i + 1) * P)
                 nc.tensor.matmul_mx(
-                    out=pre[:],
-                    lhsT=x_codes[:, g * EDGES : (g + 1) * EDGES].bitcast(FP8X4),
-                    lhsT_scale=x_scales[:, g * EDGES : (g + 1) * EDGES],
-                    rhs=w_codes[:, g * MID : (g + 1) * MID].bitcast(FP8X4),
-                    rhs_scale=w_scales[:, g * MID : (g + 1) * MID],
-                    start=(r == 0 and g == 0),
-                    stop=(r == ROUNDS - 1 and g == ROUND_PASSES - 1),
+                    out=pre[:, t, :],
+                    lhsT=w_codes[:, cols].bitcast(FP8X4),
+                    lhsT_scale=w_scales[:, cols],
+                    rhs=x_codes[kq][:, cols].bitcast(FP8X4),
+                    rhs_scale=x_scales[kq][:, cols],
+                    start=(kq == 0 and i == 0),
+                    stop=(kq == ROW_UNITS - 1 and i == UNIT_PASSES - 1),
                 )
+            if kq == ROW_UNITS - 1:
+                h_f32 = results.tile([P, EDGES], F32)
+                nc.vector.tensor_tensor(out=h_f32[:], in0=pre[:, t, :], in1=added[:, t, :], op=ADD)
+                nc.scalar.activation(out=h_grouped[:, :, t], in_=h_f32[:], func=RELU)
 
         quantised = []
-        for r in range(ROUNDS + MX_LAG):
-            if r < ROUNDS:
-                x_grouped, w_grouped = transpose_round(r)
-                quantised.append(quantise_round(x_grouped, w_grouped))
-                c, part = divmod(r, CHUNK_ROUNDS)
-                if part == CHUNK_ROUNDS - 1 and c + RAW_BUFS < CHUNKS:
-                    load_chunk(c + RAW_BUFS)
-            if r == 0:
-                prepare_biases()
-            if r >= MX_LAG:
-                multiply_round(r - MX_LAG, *quantised[r - MX_LAG])
+        for u in range(W_UNITS):
+            w_codes = codes.tile([P, K_UNIT // PACK], U32, align_bytes=64)
+            w_scales = codes.tile([P, K_UNIT // PACK], U8, align_bytes=64)
+            w_pairs = w_raw[u][:].bitcast(F32)
+            quantise_unit([w_pairs[:, j * BANK : (j + 1) * BANK] for j in range(UNIT_BANKS)], w_codes, w_scales)
+            quantised.append((w_codes, w_scales))
+            if u + W_BUFS < W_UNITS:
+                load_w_unit(u + W_BUFS)
+            if u > 0:
+                multiply_unit(u - 1, *quantised[u - 1])
+        multiply_unit(W_UNITS - 1, *quantised[W_UNITS - 1])
 
         scale_rows = W2_scales[0].rearrange("(q r) n -> r q n", r=4)
         for r in range(4):
@@ -200,13 +201,6 @@ def tile_edgenetwork_k_kernel(
         w2_codes = const.tile([P, OUT], U32, align_bytes=64)
         nc.sync.dma_start(out=w2_codes[:].bitcast(I32), in_=W2_words[0].rearrange("p n t -> p (n t)").bitcast(I32))
 
-        h_rows = const.tile([P, PACK, P], F32)
-        nc.vector.tensor_tensor(out=h_rows[:], in0=pre[:].rearrange("e (p t) -> e t p", t=PACK), in1=added[:], op=ADD)
-        h_bank = banks.tile([P, PACK, EDGES], F32, tag="bank")
-        for t in range(PACK):
-            nc.tensor.transpose(h_bank[:, t, :], h_rows[:, t, :], ident[:])
-        h_grouped = const.tile([P, EDGES, PACK], BF16, align_bytes=64)
-        nc.scalar.activation(out=h_grouped[:], in_=h_bank[:].rearrange("p t e -> p e t"), func=RELU)
         h_codes = const.tile([P, EDGES], U32, align_bytes=64)
         h_scales = const.tile([P, EDGES], U8, align_bytes=64)
         nc.vector.quantize_mx(

@@ -33,6 +33,7 @@ UNIT_PASSES = K_UNIT // K_PASS
 ROW_UNITS = NODE_K // K_UNIT
 W_UNITS = ROW_SETS * ROW_UNITS
 W_BUFS = 8
+MX_LAG = 2
 
 FLOPS = 2 * EDGES * (NODE_K + 1) * MID + 2 * EDGES * MID * OUT
 
@@ -59,7 +60,7 @@ def tile_edgenetwork_k_kernel(
         const = stack.enter_context(tc.tile_pool(name="const", bufs=1))
         raw = stack.enter_context(tc.tile_pool(name="raw", bufs=W_BUFS))
         grouped_pool = stack.enter_context(tc.tile_pool(name="grouped", bufs=3))
-        codes = stack.enter_context(tc.tile_pool(name="codes", bufs=3))
+        codes = stack.enter_context(tc.tile_pool(name="codes", bufs=MX_LAG + 2))
         results = stack.enter_context(tc.tile_pool(name="results", bufs=OUT // BANK))
         sums = stack.enter_context(tc.psum_pool(name="sums", bufs=1))
         banks = stack.enter_context(tc.psum_pool(name="banks", bufs=PSUM_BANKS - 1))
@@ -112,7 +113,7 @@ def tile_edgenetwork_k_kernel(
                 bank = banks.tile([P, 2 * BANK_PASSES, P], F32, tag="bank")
                 for b in range(2 * BANK_PASSES):
                     nc.tensor.transpose(bank[:, b, :], pairs[:, b * P : (b + 1) * P], ident[:])
-                copy = nc.vector.tensor_copy if j == 0 else nc.scalar.copy
+                copy = nc.vector.tensor_copy if j == UNIT_BANKS - 1 else nc.scalar.copy
                 copy(
                     out=grouped[:].bitcast(F32)[:, j * BANK : (j + 1) * BANK].rearrange(
                         "p (g r u) -> p g r u", g=BANK_PASSES, u=2
@@ -135,7 +136,7 @@ def tile_edgenetwork_k_kernel(
                 cols = slice(n * BANK, (n + 1) * BANK)
                 spread = banks.tile([P, BANK], F32, tag="bank")
                 nc.tensor.matmul(out=spread[:], lhsT=ones[:], rhs=b2_row[:, cols], start=True, stop=True)
-                nc.vector.tensor_copy(out=b2_all[:, cols], in_=spread[:])
+                nc.scalar.copy(out=b2_all[:, cols], in_=spread[:])
             b1_f32 = const.tile([P, ROW_SETS], F32)
             nc.vector.tensor_copy(out=b1_f32[:], in_=b1_bf[:])
             w1_edge = const.tile([P, ROW_SETS], F32)
@@ -183,17 +184,17 @@ def tile_edgenetwork_k_kernel(
                 nc.scalar.activation(out=h_grouped[:, :, t], in_=h_f32[:], func=RELU)
 
         quantised = []
-        for u in range(W_UNITS):
-            w_codes = codes.tile([P, K_UNIT // PACK], U32, align_bytes=64)
-            w_scales = codes.tile([P, K_UNIT // PACK], U8, align_bytes=64)
-            w_pairs = w_raw[u][:].bitcast(F32)
-            quantise_unit([w_pairs[:, j * BANK : (j + 1) * BANK] for j in range(UNIT_BANKS)], w_codes, w_scales)
-            quantised.append((w_codes, w_scales))
+        for u in range(W_UNITS + MX_LAG):
+            if u < W_UNITS:
+                w_codes = codes.tile([P, K_UNIT // PACK], U32, align_bytes=64)
+                w_scales = codes.tile([P, K_UNIT // PACK], U8, align_bytes=64)
+                w_pairs = w_raw[u][:].bitcast(F32)
+                quantise_unit([w_pairs[:, j * BANK : (j + 1) * BANK] for j in range(UNIT_BANKS)], w_codes, w_scales)
+                quantised.append((w_codes, w_scales))
             if u + W_BUFS < W_UNITS:
                 load_w_unit(u + W_BUFS)
-            if u > 0:
-                multiply_unit(u - 1, *quantised[u - 1])
-        multiply_unit(W_UNITS - 1, *quantised[W_UNITS - 1])
+            if u >= MX_LAG:
+                multiply_unit(u - MX_LAG, *quantised[u - MX_LAG])
 
         scale_rows = W2_scales[0].rearrange("(q r) n -> r q n", r=4)
         for r in range(4):

@@ -33,7 +33,7 @@ UNIT_PASSES = K_UNIT // K_PASS
 ROW_UNITS = NODE_K // K_UNIT
 W_UNITS = ROW_SETS * ROW_UNITS
 W_BUFS = 8
-MX_LAG = 2
+ROUND_UNITS = 2
 
 FLOPS = 2 * EDGES * (NODE_K + 1) * MID + 2 * EDGES * MID * OUT
 
@@ -60,7 +60,7 @@ def tile_edgenetwork_k_kernel(
         const = stack.enter_context(tc.tile_pool(name="const", bufs=1))
         raw = stack.enter_context(tc.tile_pool(name="raw", bufs=W_BUFS))
         grouped_pool = stack.enter_context(tc.tile_pool(name="grouped", bufs=3))
-        codes = stack.enter_context(tc.tile_pool(name="codes", bufs=MX_LAG + 2))
+        codes = stack.enter_context(tc.tile_pool(name="codes", bufs=3 * ROUND_UNITS))
         results = stack.enter_context(tc.tile_pool(name="results", bufs=OUT // BANK))
         sums = stack.enter_context(tc.psum_pool(name="sums", bufs=1))
         banks = stack.enter_context(tc.psum_pool(name="banks", bufs=PSUM_BANKS - 1))
@@ -184,17 +184,17 @@ def tile_edgenetwork_k_kernel(
                 nc.scalar.activation(out=h_grouped[:, :, t], in_=h_f32[:], func=RELU)
 
         quantised = []
-        for u in range(W_UNITS + MX_LAG):
-            if u < W_UNITS:
+        for first in range(0, W_UNITS + ROUND_UNITS, ROUND_UNITS):
+            for u in range(first, min(first + ROUND_UNITS, W_UNITS)):
                 w_codes = codes.tile([P, K_UNIT // PACK], U32, align_bytes=64)
                 w_scales = codes.tile([P, K_UNIT // PACK], U8, align_bytes=64)
                 w_pairs = w_raw[u][:].bitcast(F32)
                 quantise_unit([w_pairs[:, j * BANK : (j + 1) * BANK] for j in range(UNIT_BANKS)], w_codes, w_scales)
                 quantised.append((w_codes, w_scales))
-            if u + W_BUFS < W_UNITS:
-                load_w_unit(u + W_BUFS)
-            if u >= MX_LAG:
-                multiply_unit(u - MX_LAG, *quantised[u - MX_LAG])
+                if u + W_BUFS < W_UNITS:
+                    load_w_unit(u + W_BUFS)
+            for u in range(max(first - ROUND_UNITS, 0), first):
+                multiply_unit(u, *quantised[u])
 
         scale_rows = W2_scales[0].rearrange("(q r) n -> r q n", r=4)
         for r in range(4):

@@ -33,7 +33,7 @@ UNIT_PASSES = K_UNIT // K_PASS
 ROW_UNITS = NODE_K // K_UNIT
 W_UNITS = ROW_SETS * ROW_UNITS
 W_BUFS = 8
-ROUND_UNITS = 2
+MX_LAG = 2
 
 FLOPS = 2 * EDGES * (NODE_K + 1) * MID + 2 * EDGES * MID * OUT
 
@@ -60,14 +60,12 @@ def tile_edgenetwork_k_kernel(
         const = stack.enter_context(tc.tile_pool(name="const", bufs=1))
         raw = stack.enter_context(tc.tile_pool(name="raw", bufs=W_BUFS))
         grouped_pool = stack.enter_context(tc.tile_pool(name="grouped", bufs=3))
-        codes = stack.enter_context(tc.tile_pool(name="codes", bufs=3 * ROUND_UNITS))
+        codes = stack.enter_context(tc.tile_pool(name="codes", bufs=MX_LAG + 2))
         results = stack.enter_context(tc.tile_pool(name="results", bufs=OUT // BANK))
         sums = stack.enter_context(tc.psum_pool(name="sums", bufs=1))
         banks = stack.enter_context(tc.psum_pool(name="banks", bufs=PSUM_BANKS - 1))
         stack.enter_context(tc.manual_schedule())
 
-        edge_all = const.tile([P, EDGES], BF16)
-        nc.scalar.dma_start(out=edge_all[:], in_=edge_feat.partition_broadcast(P))
         b1_bf = const.tile([P, ROW_SETS], BF16)
         nc.scalar.dma_start(out=b1_bf[:], in_=b1.rearrange("(p t) -> p t", t=ROW_SETS))
         w1_edge_bf = const.tile([P, ROW_SETS, 1], BF16)
@@ -76,8 +74,8 @@ def tile_edgenetwork_k_kernel(
                 out=w1_edge_bf[:], in_=W1.rearrange("(p t) k -> p t k", t=ROW_SETS)[:, :, NODE_K : NODE_K + 1]
             )
 
-        b2_row = const.tile([P, OUT], BF16)
-        nc.vector.memset(b2_row[:].bitcast(I32), 0)
+        one_row = const.tile([P, OUT + BANK], BF16)
+        nc.vector.memset(one_row[:].bitcast(I32), 0)
         ones = const.tile([P, P], BF16)
         nc.vector.memset(ones[:], 1.0)
         w2_scales = const.tile([P, OUT], U8, align_bytes=64)
@@ -94,7 +92,8 @@ def tile_edgenetwork_k_kernel(
             nc.sync.dma_start(out=x_tile[:], in_=part)
             x_banks.extend([x_tile[:].bitcast(F32)[:, j * BANK : (j + 1) * BANK] for j in range(part.shape[1] // K_BANK)])
             if i == 0:
-                nc.sync.dma_start(out=b2_row[0:1, :], in_=b2.unsqueeze(0))
+                nc.sync.dma_start(out=one_row[0:1, 0:OUT], in_=b2.unsqueeze(0))
+                nc.sync.dma_start(out=one_row[0:1, OUT : OUT + EDGES], in_=edge_feat.unsqueeze(0))
 
         w_raw = []
 
@@ -128,15 +127,17 @@ def tile_edgenetwork_k_kernel(
                     in_=grouped[:, half * K_UNIT // 2 : (half + 1) * K_UNIT // 2],
                 )
 
-        b2_all = const.tile([P, OUT], BF16)
+        every_row = const.tile([P, OUT + BANK], BF16)
+        b2_all = every_row[:, 0:OUT]
+        edge_all = every_row[:, OUT : OUT + EDGES]
         added = const.tile([P, ROW_SETS, EDGES], F32)
 
         def prepare_biases():
-            for n in range(OUT // BANK):
+            for n in range(OUT // BANK + 1):
                 cols = slice(n * BANK, (n + 1) * BANK)
                 spread = banks.tile([P, BANK], F32, tag="bank")
-                nc.tensor.matmul(out=spread[:], lhsT=ones[:], rhs=b2_row[:, cols], start=True, stop=True)
-                nc.scalar.copy(out=b2_all[:, cols], in_=spread[:])
+                nc.tensor.matmul(out=spread[:], lhsT=ones[:], rhs=one_row[:, cols], start=True, stop=True)
+                nc.scalar.copy(out=every_row[:, cols], in_=spread[:])
             b1_f32 = const.tile([P, ROW_SETS], F32)
             nc.vector.tensor_copy(out=b1_f32[:], in_=b1_bf[:])
             w1_edge = const.tile([P, ROW_SETS], F32)
@@ -144,7 +145,7 @@ def tile_edgenetwork_k_kernel(
             for t in range(ROW_SETS):
                 nc.vector.tensor_scalar(
                     out=added[:, t, :],
-                    in0=edge_all[:],
+                    in0=edge_all,
                     scalar1=w1_edge[:, t : t + 1],
                     scalar2=b1_f32[:, t : t + 1],
                     op0=MULT,
@@ -184,23 +185,26 @@ def tile_edgenetwork_k_kernel(
                 nc.scalar.activation(out=h_grouped[:, :, t], in_=h_f32[:], func=RELU)
 
         quantised = []
-        for first in range(0, W_UNITS + ROUND_UNITS, ROUND_UNITS):
-            for u in range(first, min(first + ROUND_UNITS, W_UNITS)):
+        for u in range(W_UNITS + MX_LAG):
+            if u < W_UNITS:
                 w_codes = codes.tile([P, K_UNIT // PACK], U32, align_bytes=64)
                 w_scales = codes.tile([P, K_UNIT // PACK], U8, align_bytes=64)
                 w_pairs = w_raw[u][:].bitcast(F32)
                 quantise_unit([w_pairs[:, j * BANK : (j + 1) * BANK] for j in range(UNIT_BANKS)], w_codes, w_scales)
                 quantised.append((w_codes, w_scales))
-                if u + W_BUFS < W_UNITS:
-                    load_w_unit(u + W_BUFS)
-            for u in range(max(first - ROUND_UNITS, 0), first):
-                multiply_unit(u, *quantised[u])
+            if u + W_BUFS < W_UNITS:
+                load_w_unit(u + W_BUFS)
+            if u >= MX_LAG:
+                multiply_unit(u - MX_LAG, *quantised[u - MX_LAG])
 
         scale_rows = W2_scales[0].rearrange("(q r) n -> r q n", r=4)
         for r in range(4):
             nc.sync.dma_start(out=w2_scales[r:P:32, :].bitcast(I32), in_=scale_rows[r].bitcast(I32))
         w2_codes = const.tile([P, OUT], U32, align_bytes=64)
-        nc.sync.dma_start(out=w2_codes[:].bitcast(I32), in_=W2_words[0].rearrange("p n t -> p (n t)").bitcast(I32))
+        w2_words = W2_words[0].rearrange("p n t -> p (n t)").bitcast(I32)
+        for n in range(OUT // BANK):
+            cols = slice(n * BANK, (n + 1) * BANK)
+            nc.sync.dma_start(out=w2_codes[:, cols].bitcast(I32), in_=w2_words[:, cols])
 
         h_codes = const.tile([P, EDGES], U32, align_bytes=64)
         h_scales = const.tile([P, EDGES], U8, align_bytes=64)

@@ -32,6 +32,7 @@ K_UNIT = UNIT_BANKS * K_BANK
 UNIT_PASSES = K_UNIT // K_PASS
 ROW_UNITS = NODE_K // K_UNIT
 W_UNITS = ROW_SETS * ROW_UNITS
+NARROW = 32
 W_BUFS = 8
 MX_LAG = 2
 
@@ -66,15 +67,7 @@ def tile_edgenetwork_k_kernel(
         banks = stack.enter_context(tc.psum_pool(name="banks", bufs=PSUM_BANKS - 1))
         stack.enter_context(tc.manual_schedule())
 
-        b1_bf = const.tile([P, ROW_SETS], BF16)
-        nc.scalar.dma_start(out=b1_bf[:], in_=b1.rearrange("(p t) -> p t", t=ROW_SETS))
-        w1_edge_bf = const.tile([P, ROW_SETS, 1], BF16)
-        with nc.allow_non_contiguous_dma(reason="one column of W1: 512 single elements"):
-            nc.scalar.dma_start(
-                out=w1_edge_bf[:], in_=W1.rearrange("(p t) k -> p t k", t=ROW_SETS)[:, :, NODE_K : NODE_K + 1]
-            )
-
-        one_row = const.tile([P, OUT + BANK], BF16)
+        one_row = const.tile([P, OUT + BANK + MID], BF16)
         nc.vector.memset(one_row[:].bitcast(I32), 0)
         ones = const.tile([P, P], BF16)
         nc.vector.memset(ones[:], 1.0)
@@ -94,13 +87,15 @@ def tile_edgenetwork_k_kernel(
             if i == 0:
                 nc.sync.dma_start(out=one_row[0:1, 0:OUT], in_=b2.unsqueeze(0))
                 nc.sync.dma_start(out=one_row[0:1, OUT : OUT + EDGES], in_=edge_feat.unsqueeze(0))
+                nc.sync.dma_start(out=one_row[0:1, OUT + BANK : OUT + BANK + MID], in_=b1.unsqueeze(0))
 
         w_raw = []
 
         def load_w_unit(u):
             t, kq = divmod(u, ROW_UNITS)
-            w_tile = raw.tile([P, K_UNIT], BF16)
-            nc.sync.dma_start(out=w_tile[:], in_=w1_sets[t][:, kq * K_UNIT : (kq + 1) * K_UNIT])
+            width = K_UNIT + 1 if kq == ROW_UNITS - 1 else K_UNIT
+            w_tile = raw.tile([P, K_UNIT + 2], BF16)
+            nc.sync.dma_start(out=w_tile[:, 0:width], in_=w1_sets[t][:, kq * K_UNIT : kq * K_UNIT + width])
             w_raw.append(w_tile)
 
         for u in range(W_BUFS):
@@ -131,6 +126,7 @@ def tile_edgenetwork_k_kernel(
         b2_all = every_row[:, 0:OUT]
         edge_all = every_row[:, OUT : OUT + EDGES]
         added = const.tile([P, ROW_SETS, EDGES], F32)
+        b1_f32 = const.tile([P, ROW_SETS], F32)
 
         def prepare_biases():
             for n in range(OUT // BANK + 1):
@@ -138,19 +134,28 @@ def tile_edgenetwork_k_kernel(
                 spread = banks.tile([P, BANK], F32, tag="bank")
                 nc.tensor.matmul(out=spread[:], lhsT=ones[:], rhs=one_row[:, cols], start=True, stop=True)
                 nc.scalar.copy(out=every_row[:, cols], in_=spread[:])
-            b1_f32 = const.tile([P, ROW_SETS], F32)
-            nc.vector.tensor_copy(out=b1_f32[:], in_=b1_bf[:])
-            w1_edge = const.tile([P, ROW_SETS], F32)
-            nc.vector.tensor_copy(out=w1_edge[:], in_=w1_edge_bf[:, :, 0])
+            b1_bank = banks.tile([P, ROW_SETS, NARROW], F32, tag="bank")
             for t in range(ROW_SETS):
-                nc.vector.tensor_scalar(
-                    out=added[:, t, :],
-                    in0=edge_all,
-                    scalar1=w1_edge[:, t : t + 1],
-                    scalar2=b1_f32[:, t : t + 1],
-                    op0=MULT,
-                    op1=ADD,
+                nc.tensor.matmul(
+                    out=b1_bank[:, t, :],
+                    lhsT=one_row[:, OUT + BANK + t : OUT + BANK + MID : ROW_SETS],
+                    rhs=ones[:, 0:NARROW],
+                    start=True,
+                    stop=True,
                 )
+            nc.scalar.copy(out=b1_f32[:], in_=b1_bank[:, :, 0])
+
+        def prepare_added(t, w_tile):
+            w1_edge = results.tile([P, 1], F32)
+            nc.vector.tensor_copy(out=w1_edge[:], in_=w_tile[:, K_UNIT : K_UNIT + 1])
+            nc.vector.tensor_scalar(
+                out=added[:, t, :],
+                in0=edge_all,
+                scalar1=w1_edge[:],
+                scalar2=b1_f32[:, t : t + 1],
+                op0=MULT,
+                op1=ADD,
+            )
 
         x_codes = []
         x_scales = []
@@ -189,7 +194,9 @@ def tile_edgenetwork_k_kernel(
             if u < W_UNITS:
                 w_codes = codes.tile([P, K_UNIT // PACK], U32, align_bytes=64)
                 w_scales = codes.tile([P, K_UNIT // PACK], U8, align_bytes=64)
-                w_pairs = w_raw[u][:].bitcast(F32)
+                w_pairs = w_raw[u][:, 0:K_UNIT].bitcast(F32)
+                if u % ROW_UNITS == ROW_UNITS - 1:
+                    prepare_added(u // ROW_UNITS, w_raw[u])
                 quantise_unit([w_pairs[:, j * BANK : (j + 1) * BANK] for j in range(UNIT_BANKS)], w_codes, w_scales)
                 quantised.append((w_codes, w_scales))
             if u + W_BUFS < W_UNITS:

from contextlib import ExitStack

import concourse.mybir as mybir
from concourse.masks import make_identity

F32 = mybir.dt.float32
BF16 = mybir.dt.bfloat16
I32 = mybir.dt.int32
U32 = mybir.dt.uint32
U8 = mybir.dt.uint8
FP8X4 = mybir.dt.float8_e4m3fn_x4
ADD = mybir.AluOpType.add
MULT = mybir.AluOpType.mult
RELU = mybir.ActivationFunctionType.Relu
TANH = mybir.ActivationFunctionType.Tanh

P = 128
PACK = 4
K_PASS = P * PACK
EDGES = 128
NODE_K = 16384
MID = 512
OUT = 2048
ROW_SETS = MID // P
BANK = 512
PSUM_BANKS = 8

K_BANK = 2 * BANK
BANK_PASSES = K_BANK // K_PASS
UNIT_BANKS = 4
K_UNIT = UNIT_BANKS * K_BANK
UNIT_PASSES = K_UNIT // K_PASS
ROW_UNITS = NODE_K // K_UNIT
W_UNITS = ROW_SETS * ROW_UNITS
NARROW = 32
W_BUFS = 8
MX_LAG = 2

FLOPS = 2 * EDGES * (NODE_K + 1) * MID + 2 * EDGES * MID * OUT


def tile_edgenetwork_k_kernel(
    tc,
    dst_node_feat,
    dst_node_hidden,
    src_node_feat,
    src_node_hidden,
    edge_feat,
    W1,
    b1,
    W2_words,
    W2_scales,
    b2,
    out,
):
    nc = tc.nc
    node_inputs = (dst_node_feat, dst_node_hidden, src_node_feat, src_node_hidden)
    w1_sets = W1.rearrange("(p t) k -> t p k", t=ROW_SETS)

    with ExitStack() as stack:
        const = stack.enter_context(tc.tile_pool(name="const", bufs=1))
        raw = stack.enter_context(tc.tile_pool(name="raw", bufs=W_BUFS))
        grouped_pool = stack.enter_context(tc.tile_pool(name="grouped", bufs=3))
        codes = stack.enter_context(tc.tile_pool(name="codes", bufs=MX_LAG + 2))
        results = stack.enter_context(tc.tile_pool(name="results", bufs=OUT // BANK))
        sums = stack.enter_context(tc.psum_pool(name="sums", bufs=1))
        banks = stack.enter_context(tc.psum_pool(name="banks", bufs=PSUM_BANKS - 1))
        stack.enter_context(tc.manual_schedule())

        one_row = const.tile([P, OUT + BANK + MID], BF16)
        nc.vector.memset(one_row[:].bitcast(I32), 0)
        ones = const.tile([P, P], BF16)
        nc.vector.memset(ones[:], 1.0)
        w2_scales = const.tile([P, OUT], U8, align_bytes=64)
        nc.vector.memset(w2_scales[:].bitcast(I32), 0)
        warm = const.tile([P, 1], F32)
        nc.vector.memset(warm[:], 0.0)
        nc.scalar.activation(out=warm[:], in_=warm[:], func=TANH)
        ident = const.tile([P, P], F32)
        make_identity(nc, ident[:])

        x_banks = []
        for i, part in enumerate(node_inputs):
            x_tile = const.tile([P, part.shape[1]], BF16, name="x_raw%d" % i)
            nc.sync.dma_start(out=x_tile[:], in_=part)
            x_banks.extend([x_tile[:].bitcast(F32)[:, j * BANK : (j + 1) * BANK] for j in range(part.shape[1] // K_BANK)])
            if i == 0:
                nc.sync.dma_start(out=one_row[0:1, 0:OUT], in_=b2.unsqueeze(0))
                nc.sync.dma_start(out=one_row[0:1, OUT : OUT + EDGES], in_=edge_feat.unsqueeze(0))
                nc.sync.dma_start(out=one_row[0:1, OUT + BANK : OUT + BANK + MID], in_=b1.unsqueeze(0))

        w_raw = []

        def load_w_unit(u):
            t, kq = divmod(u, ROW_UNITS)
            width = K_UNIT + 1 if kq == ROW_UNITS - 1 else K_UNIT
            w_tile = raw.tile([P, K_UNIT + 2], BF16)
            nc.sync.dma_start(out=w_tile[:, 0:width], in_=w1_sets[t][:, kq * K_UNIT : kq * K_UNIT + width])
            w_raw.append(w_tile)

        for u in range(W_BUFS):
            load_w_unit(u)

        def quantise_unit(bank_pairs, unit_codes, unit_scales):
            grouped = grouped_pool.tile([P, K_UNIT], BF16, align_bytes=64)
            for j, pairs in enumerate(bank_pairs):
                bank = banks.tile([P, 2 * BANK_PASSES, P], F32, tag="bank")
                for b in range(2 * BANK_PASSES):
                    nc.tensor.transpose(bank[:, b, :], pairs[:, b * P : (b + 1) * P], ident[:])
                copy = nc.vector.tensor_copy if j == UNIT_BANKS - 1 else nc.scalar.copy
                copy(
                    out=grouped[:].bitcast(F32)[:, j * BANK : (j + 1) * BANK].rearrange(
                        "p (g r u) -> p g r u", g=BANK_PASSES, u=2
                    ),
                    in_=bank[:].rearrange("p (g u) r -> p g r u", u=2),
                )
            for half in range(2):
                words = slice(half * K_UNIT // PACK // 2, (half + 1) * K_UNIT // PACK // 2)
                nc.vector.quantize_mx(
                    out=unit_codes[:, words].bitcast(FP8X4),
                    scales=unit_scales[:, words],
                    in_=grouped[:, half * K_UNIT // 2 : (half + 1) * K_UNIT // 2],
                )

        every_row = const.tile([P, OUT + BANK], BF16)
        b2_all = every_row[:, 0:OUT]
        edge_all = every_row[:, OUT : OUT + EDGES]
        added = const.tile([P, ROW_SETS, EDGES], F32)
        b1_f32 = const.tile([P, ROW_SETS], F32)

        def prepare_biases():
            for n in range(OUT // BANK + 1):
                cols = slice(n * BANK, (n + 1) * BANK)
                spread = banks.tile([P, BANK], F32, tag="bank")
                nc.tensor.matmul(out=spread[:], lhsT=ones[:], rhs=one_row[:, cols], start=True, stop=True)
                nc.scalar.copy(out=every_row[:, cols], in_=spread[:])
            b1_bank = banks.tile([P, ROW_SETS, NARROW], F32, tag="bank")
            for t in range(ROW_SETS):
                nc.tensor.matmul(
                    out=b1_bank[:, t, :],
                    lhsT=one_row[:, OUT + BANK + t : OUT + BANK + MID : ROW_SETS],
                    rhs=ones[:, 0:NARROW],
                    start=True,
                    stop=True,
                )
            nc.scalar.copy(out=b1_f32[:], in_=b1_bank[:, :, 0])

        def prepare_added(t, w_tile):
            w1_edge = results.tile([P, 1], F32)
            nc.vector.tensor_copy(out=w1_edge[:], in_=w_tile[:, K_UNIT : K_UNIT + 1])
            nc.vector.tensor_scalar(
                out=added[:, t, :],
                in0=edge_all,
                scalar1=w1_edge[:],
                scalar2=b1_f32[:, t : t + 1],
                op0=MULT,
                op1=ADD,
            )

        x_codes = []
        x_scales = []
        for kq in range(ROW_UNITS):
            x_unit_codes = const.tile([P, K_UNIT // PACK], U32, name="x_codes%d" % kq, align_bytes=64)
            x_unit_scales = const.tile([P, K_UNIT // PACK], U8, name="x_scales%d" % kq, align_bytes=64)
            quantise_unit(x_banks[kq * UNIT_BANKS : (kq + 1) * UNIT_BANKS], x_unit_codes, x_unit_scales)
            x_codes.append(x_unit_codes)
            x_scales.append(x_unit_scales)
            if kq == 0:
                prepare_biases()

        pre = sums.tile([P, ROW_SETS, EDGES], F32)
        h_grouped = const.tile([P, EDGES, PACK], BF16, align_bytes=64)

        def multiply_unit(u, w_codes, w_scales):
            t, kq = divmod(u, ROW_UNITS)
            for i in range(UNIT_PASSES):
                cols = slice(i * P, (i + 1) * P)
                nc.tensor.matmul_mx(
                    out=pre[:, t, :],
                    lhsT=w_codes[:, cols].bitcast(FP8X4),
                    lhsT_scale=w_scales[:, cols],
                    rhs=x_codes[kq][:, cols].bitcast(FP8X4),
                    rhs_scale=x_scales[kq][:, cols],
                    start=(kq == 0 and i == 0),
                    stop=(kq == ROW_UNITS - 1 and i == UNIT_PASSES - 1),
                )
            if kq == ROW_UNITS - 1:
                h_f32 = results.tile([P, EDGES], F32)
                nc.vector.tensor_tensor(out=h_f32[:], in0=pre[:, t, :], in1=added[:, t, :], op=ADD)
                nc.scalar.activation(out=h_grouped[:, :, t], in_=h_f32[:], func=RELU)

        quantised = []
        for u in range(W_UNITS + MX_LAG):
            if u < W_UNITS:
                w_codes = codes.tile([P, K_UNIT // PACK], U32, align_bytes=64)
                w_scales = codes.tile([P, K_UNIT // PACK], U8, align_bytes=64)
                w_pairs = w_raw[u][:, 0:K_UNIT].bitcast(F32)
                if u % ROW_UNITS == ROW_UNITS - 1:
                    prepare_added(u // ROW_UNITS, w_raw[u])
                quantise_unit([w_pairs[:, j * BANK : (j + 1) * BANK] for j in range(UNIT_BANKS)], w_codes, w_scales)
                quantised.append((w_codes, w_scales))
            if u + W_BUFS < W_UNITS:
                load_w_unit(u + W_BUFS)
            if u >= MX_LAG:
                multiply_unit(u - MX_LAG, *quantised[u - MX_LAG])

        scale_rows = W2_scales[0].rearrange("(q r) n -> r q n", r=4)
        for r in range(4):
            nc.sync.dma_start(out=w2_scales[r:P:32, :].bitcast(I32), in_=scale_rows[r].bitcast(I32))
        w2_codes = const.tile([P, OUT], U32, align_bytes=64)
        w2_words = W2_words[0].rearrange("p n t -> p (n t)").bitcast(I32)
        for n in range(OUT // BANK):
            cols = slice(n * BANK, (n + 1) * BANK)
            nc.sync.dma_start(out=w2_codes[:, cols].bitcast(I32), in_=w2_words[:, cols])

        h_codes = const.tile([P, EDGES], U32, align_bytes=64)
        h_scales = const.tile([P, EDGES], U8, align_bytes=64)
        nc.vector.quantize_mx(
            out=h_codes[:].bitcast(FP8X4), scales=h_scales[:], in_=h_grouped[:].rearrange("p e t -> p (e t)")
        )

        for n in range(OUT // BANK):
            cols = slice(n * BANK, (n + 1) * BANK)
            product = banks.tile([P, BANK], F32, tag="bank")
            nc.tensor.matmul_mx(
                out=product[:],
                lhsT=h_codes[:].bitcast(FP8X4),
                lhsT_scale=h_scales[:],
                rhs=w2_codes[:, cols].bitcast(FP8X4),
                rhs_scale=w2_scales[:, cols],
                start=True,
                stop=True,
            )
            biased = results.tile([P, BANK], F32)
            nc.vector.tensor_tensor(out=biased[:], in0=product[:], in1=b2_all[:, cols], op=ADD)
            y = results.tile([P, BANK], F32)
            nc.scalar.activation(out=y[:], in_=biased[:], func=TANH)
            nc.sync.dma_start(out=out[:, cols], in_=y[:])
